import numpy as np
import ml_dtypes


def mxq(x, axis, fmt="e4m3"):
    dtype, down = {"e4m3": (ml_dtypes.float8_e4m3fn, 7), "e5m2": (ml_dtypes.float8_e5m2, 14)}[fmt]
    v = np.moveaxis(np.asarray(x, np.float32).astype(ml_dtypes.bfloat16).astype(np.float64), axis, -1)
    blocks = v.reshape(v.shape[:-1] + (-1, 32))
    amax = np.abs(blocks).max(-1, keepdims=True)
    byte = np.maximum(np.where(amax > 0, np.frexp(amax)[1] - 1 + 127, 0) - down, 1)
    scale = np.exp2(byte - 127.0)
    codes = (blocks / scale).astype(np.float32).astype(dtype).astype(np.float64)
    return np.moveaxis((codes * scale).reshape(v.shape), -1, axis)


WIDE = False


def mx_kscale(k):
    if not WIDE:
        return np.ones(k)
    levels = np.array([10, -10, 5, -5, 0])
    a = np.random.permutation(np.resize(levels, k // 512 * 4)).reshape(k // 512, 4)
    idx = np.arange(k)
    return np.exp2(a[idx // 512, idx % 128 // 32])


BF16 = ml_dtypes.bfloat16


def bf(x):
    return np.asarray(x, np.float32).astype(BF16)


def f64(x):
    return np.asarray(x).astype(np.float64)


B, C, H, W, M, O = 32, 512, 16, 16, 512, 128
N = B * H * W
L2_EPS = 1e-12
BN_EPS = 1e-5


def l2_normalize(x, axis):
    n = np.sqrt(np.sum(x * x, axis=axis, keepdims=True))
    return x / np.maximum(n, L2_EPS)


def setup_inputs():
    s = mx_kscale(C)
    cm = (np.random.standard_normal((N, C)) * 5.0 + np.random.standard_normal((1, C)) * 1.5) / np.sqrt(C)
    w = np.random.standard_normal((O, 2 * C)) * 0.1 / np.sqrt(2 * C)
    w[:, C:] = w[:, C:] / s
    return {"query": bf(np.random.standard_normal((B, C, H, W))), "concat_memory": bf(cm * s), "conv_w": bf(w),
            "bn_gamma": bf(1.0 + 0.1 * np.random.standard_normal(O)), "bn_beta": bf(0.2 * np.random.standard_normal(O))}


def reference(query, concat_memory, conv_w, bn_gamma, bn_beta):
    q_flat = l2_normalize(f64(query), 1).transpose(0, 2, 3, 1).reshape(N, C)
    upd = np.concatenate([q_flat, f64(concat_memory)], axis=1)
    y = mxq(upd, 1, "e4m3") @ mxq(f64(conv_w), 1, "e4m3").T
    y = y.reshape(B, H, W, O).transpose(0, 3, 1, 2)
    mean = np.mean(y, axis=(0, 2, 3), keepdims=True)
    var = np.mean((y - mean) ** 2, axis=(0, 2, 3), keepdims=True)
    y = (y - mean) / np.sqrt(var + BN_EPS)
    y = y * f64(bn_gamma)[None, :, None, None] + f64(bn_beta)[None, :, None, None]
    return np.maximum(y, 0.0)

@@ -1,0 +1,252 @@
+from contextlib import ExitStack
+
+import concourse.mybir as mybir
+from concourse.masks import make_identity
+
+F32 = mybir.dt.float32
+BF16 = mybir.dt.bfloat16
+U32 = mybir.dt.uint32
+U8 = mybir.dt.uint8
+FP8X4 = mybir.dt.float8_e4m3fn_x4
+AF = mybir.ActivationFunctionType
+ALU = mybir.AluOpType
+
+P = 128
+NG = 16
+FLOPS = 2 * 8192 * 1024 * 128
+
+L2_EPS = 1e-12
+BN_EPS = 1e-5
+SQRT_GUARD = 1e-30
+
+PINNED = True
+
+
+def tile_memory_sup_pb_t_kernel(tc, query, concat_memory, conv_w, bn_gamma, bn_beta, out):
+    nc = tc.nc
+    q_v = query.rearrange("(g b) (p j) h w -> g p b (j h w)", b=2, j=4)
+    m_v = concat_memory.rearrange("(g b p t) k -> g p b (t k)", b=2, p=P, t=2)
+    o_v = out.rearrange("(g b) o h w -> g o b (h w)", b=2)
+
+    with ExitStack() as ctx:
+        if PINNED:
+            ctx.enter_context(tc.manual_schedule())
+        const = ctx.enter_context(tc.tile_pool(name="const", bufs=1))
+        keep = ctx.enter_context(tc.tile_pool(name="keep", bufs=1))
+        xpool = ctx.enter_context(tc.tile_pool(name="xpool", bufs=7))
+        mpool = ctx.enter_context(tc.tile_pool(name="mpool", bufs=4))
+        gqpool = ctx.enter_context(tc.tile_pool(name="gqpool", bufs=2))
+        gmpool = ctx.enter_context(tc.tile_pool(name="gmpool", bufs=3))
+        jpool = ctx.enter_context(tc.tile_pool(name="jpool", bufs=2))
+        spool = ctx.enter_context(tc.tile_pool(name="spool", bufs=6))
+        psum = ctx.enter_context(tc.psum_pool(name="psum", bufs=2))
+
+        xq = {}
+        mm = {}
+        t1 = {}
+        mt = {}
+        ss = {}
+        nrm = {}
+        rr = {}
+        rbk = {}
+        gq = {}
+        gm = {}
+        qc = {}
+        qs = {}
+        mc = {}
+        ms = {}
+        yb = {}
+
+        guard = const.tile([P, 1], F32, name="guard")
+        nc.vector.memset(guard[:], SQRT_GUARD)
+        bneps = const.tile([P, 1], F32, name="bneps")
+        nc.vector.memset(bneps[:], BN_EPS)
+        warm = const.tile([P, 1], F32, name="warm")
+        nc.scalar.activation(out=warm[:], in_=bneps[:], func=AF.Sqrt)
+        ident = const.tile([P, P], F32, name="ident")
+        make_identity(nc, ident[:])
+        gam_b = const.tile([P, 1], BF16, name="gam_b")
+        bet_b = const.tile([P, 1], BF16, name="bet_b")
+        with nc.allow_non_contiguous_dma(reason="one bn parameter per partition"):
+            nc.gpsimd.dma_start(out=gam_b[:], in_=bn_gamma.rearrange("(o one) -> o one", one=1))
+            nc.gpsimd.dma_start(out=bet_b[:], in_=bn_beta.rearrange("(o one) -> o one", one=1))
+        gam = const.tile([P, 1], F32, name="gam")
+        bet = const.tile([P, 1], F32, name="bet")
+        stats = const.tile([P, NG, 6], F32, name="stats")
+        wsb = const.tile([P, 1024], BF16, name="wsb")
+        gw = const.tile([P, 2, P, 4], BF16, name="gw", align_bytes=64)
+        wc = const.tile([P, 2 * P], U32, name="wc", align_bytes=64)
+        ws = const.tile([P, 2 * P], U8, name="ws", align_bytes=64)
+
+        def load_x(g):
+            xq[g] = xpool.tile([P, 2, 4, 256], BF16, name="xq")
+            nc.sync.dma_start(out=xq[g][:].rearrange("p b j n -> p b (j n)"), in_=q_v[g])
+
+        def load_m(g):
+            mm[g] = mpool.tile([P, 2, 2, 512], BF16, name="mm")
+            nc.sync.dma_start(out=mm[g][:].rearrange("p b t k -> p b (t k)"), in_=m_v[g])
+
+        def load_w():
+            nc.sync.dma_start(out=wsb[:], in_=conv_w)
+
+        def prep_w():
+            w32 = wsb[:].bitcast(F32)
+            wps = psum.tile([P, 4, P], F32, name="wps", tag="y")
+            for h in range(2):
+                nc.tensor.transpose(wps[:, h, :], w32[:, h:256:2], ident[:])
+            for u in range(2):
+                nc.tensor.transpose(wps[:, 2 + u, :], w32[:, 256 + P * u:256 + P * u + P], ident[:])
+            nc.vector.tensor_copy(out=gw[:].bitcast(F32), in_=wps[:].rearrange("p (a h) o -> p a o h", a=2))
+            nc.vector.quantize_mx(out=wc[:].bitcast(FP8X4), scales=ws[:], in_=gw[:].rearrange("p a o t -> p (a o t)"))
+
+        def do_t1(g, b):
+            t1[(g, b)] = psum.tile([P, 4, P], F32, name="t1", tag="t1")
+            x32 = xq[g][:].bitcast(F32)
+            for j in range(4):
+                nc.tensor.transpose(t1[(g, b)][:, j, :], x32[:, b, j, :], ident[:])
+
+        def do_sq(g, b):
+            if b == 0:
+                ss[g] = spool.tile([P, 4], F32, name="ss")
+            tb = t1[(g, b)][:].bitcast(BF16).rearrange("w j (p e) -> w j p e", e=2)
+            for e in range(2):
+                junk = jpool.tile([P, 4, P], BF16, name="junk")
+                nc.scalar.activation(out=junk[:], in_=tb[:, :, :, e], func=AF.Square,
+                                     accum_out=ss[g][:, 2 * b + e:2 * b + e + 1])
+
+        def do_sqrt(g):
+            nrm[g] = spool.tile([P, 4], F32, name="nrm")
+            nc.scalar.activation(out=nrm[g][:], in_=ss[g][:], func=AF.Sqrt, bias=guard[:, 0:1])
+
+        def do_rc(g):
+            rm = spool.tile([P, 4], F32, name="rm")
+            nc.vector.tensor_scalar_max(out=rm[:], in0=nrm[g][:], scalar1=L2_EPS)
+            rr[g] = spool.tile([P, 4], F32, name="rr")
+            nc.vector.reciprocal(out=rr[g][:], in_=rm[:])
+
+        def do_rb(g):
+            rbk[g] = psum.tile([P, 2, 2, P], F32, name="rbk", tag="rb")
+            for b in range(2):
+                for e in range(2):
+                    c = 2 * b + e
+                    nc.tensor.transpose(rbk[g][:, b, e, :], rr[g][:, c:c + 1].to_broadcast([P, P]), ident[:])
+
+        def do_bm(g, b):
+            if b == 0:
+                gq[g] = gqpool.tile([P, 2, 256, 4], BF16, name="gq", align_bytes=64)
+            nc.vector.tensor_tensor(
+                out=gq[g][:, b].rearrange("p (w e) j -> p w e j", e=2),
+                in0=xq[g][:, b].rearrange("p j (w e) -> p w e j", e=2),
+                in1=rbk[g][:, b].rearrange("p e w -> p w e").unsqueeze(3).to_broadcast([P, P, 2, 4]),
+                op=ALU.mult,
+            )
+
+        def do_qq(g):
+            qc[g] = keep.tile([P, 512], U32, name="qc%d" % g, align_bytes=64)
+            qs[g] = keep.tile([P, 512], U8, name="qs%d" % g, align_bytes=64)
+            nc.vector.quantize_mx(out=qc[g][:].bitcast(FP8X4), scales=qs[g][:],
+                                  in_=gq[g][:].rearrange("p b n j -> p (b n j)"))
+
+        def do_m1(g, b):
+            mt[(g, b)] = psum.tile([P, 2, 2, P], F32, name="mt", tag="mt")
+            m32 = mm[g][:].bitcast(F32)
+            for t in range(2):
+                for u in range(2):
+                    nc.tensor.transpose(mt[(g, b)][:, u, t, :], m32[:, b, t, P * u:P * u + P], ident[:])
+
+        def do_me(g, b):
+            if b == 0:
+                gm[g] = gmpool.tile([P, 2, 256, 4], BF16, name="gm", align_bytes=64)
+            nc.scalar.copy(
+                out=gm[g][:].bitcast(F32)[:, b].rearrange("p (r t) u -> p r t u", t=2),
+                in_=mt[(g, b)][:].rearrange("p u t r -> p r t u"),
+            )
+
+        def do_qm(g):
+            mc[g] = keep.tile([P, 512], U32, name="mc%d" % g, align_bytes=64)
+            ms[g] = keep.tile([P, 512], U8, name="ms%d" % g, align_bytes=64)
+            nc.vector.quantize_mx(out=mc[g][:].bitcast(FP8X4), scales=ms[g][:],
+                                  in_=gm[g][:].rearrange("p b n j -> p (b n j)"))
+
+        def do_mx(g, tag):
+            yb[g] = psum.tile([P, 512], F32, name="yb", tag=tag)
+            nc.tensor.matmul_mx(out=yb[g][:], lhsT=wc[:, 0:P].bitcast(FP8X4), lhsT_scale=ws[:, 0:P],
+                                rhs=qc[g][:].bitcast(FP8X4), rhs_scale=qs[g][:], start=True, stop=False)
+            nc.tensor.matmul_mx(out=yb[g][:], lhsT=wc[:, P:2 * P].bitcast(FP8X4), lhsT_scale=ws[:, P:2 * P],
+                                rhs=mc[g][:].bitcast(FP8X4), rhs_scale=ms[g][:], start=False, stop=True)
+
+        def do_bs(g):
+            nc.vector.bn_stats(out=stats[:, g, :], in_=yb[g][:])
+
+        def ok(g):
+            return 0 <= g < NG
+
+        first_tag = {12: "t1", 13: "t1", 14: "mt", 15: "mt"}
+
+        for i in range(-7, NG):
+            if ok(i + 6):
+                load_m(i + 6)
+            if i == -6:
+                load_w()
+            if ok(i + 7):
+                load_x(i + 7)
+            if ok(i):
+                do_mx(i, first_tag.get(i, "y"))
+            if i == 14:
+                do_mx(0, "rb")
+            if i == 15:
+                do_mx(1, "rb")
+            for b in range(2):
+                if ok(i + 4):
+                    do_t1(i + 4, b)
+                    do_sq(i + 4, b)
+                if ok(i + 3):
+                    do_m1(i + 3, b)
+                    do_me(i + 3, b)
+                if ok(i + 1):
+                    do_bm(i + 1, b)
+                if b == 0:
+                    if ok(i + 2):
+                        do_rc(i + 2)
+                        do_rb(i + 2)
+            if i == -4:
+                prep_w()
+            if ok(i + 4):
+                do_sqrt(i + 4)
+            if ok(i):
+                do_bs(i)
+            if i == 2:
+                nc.vector.tensor_copy(out=gam[:], in_=gam_b[:])
+                nc.vector.tensor_copy(out=bet[:], in_=bet_b[:])
+            if ok(i + 2):
+                do_qm(i + 2)
+            if ok(i + 1):
+                do_qq(i + 1)
+
+        mv = const.tile([P, 2], F32, name="mv")
+        nc.vector.bn_aggr(out=mv[:], in_=stats[:].rearrange("p g s -> p (g s)"))
+        sd = const.tile([P, 1], F32, name="sd")
+        nc.scalar.activation(out=sd[:], in_=mv[:, 1:2], func=AF.Sqrt, bias=bneps[:, 0:1])
+        rs = const.tile([P, 1], F32, name="rs")
+        nc.vector.reciprocal(out=rs[:], in_=sd[:])
+        sc = const.tile([P, 1], F32, name="sc")
+        nc.vector.tensor_tensor(out=sc[:], in0=rs[:], in1=gam[:], op=ALU.mult)
+        nb = const.tile([P, 1], F32, name="nb")
+        nc.vector.tensor_scalar(out=nb[:], in0=mv[:, 0:1], scalar1=sc[:, 0:1], scalar2=-1.0,
+                                op0=ALU.mult, op1=ALU.mult)
+        bi = const.tile([P, 1], F32, name="bi")
+        nc.vector.tensor_tensor(out=bi[:], in0=nb[:], in1=bet[:], op=ALU.add)
+
+        order = [10, 11, 12, 13, 14, 15, 0, 1, 2, 3, 4, 5, 6, 7, 8, 9]
+        refill = ["y", "y", "t1", "t1", "mt", "mt", "rb", "rb"]
+        for n, g in enumerate(order):
+            st = keep.tile([P, 512], F32, name="st%d" % g)
+            if n % 3 == 1:
+                nc.vector.tensor_scalar(out=st[:], in0=yb[g][:], scalar1=sc[:, 0:1], scalar2=bi[:, 0:1],
+                                        op0=ALU.mult, op1=ALU.add)
+                nc.vector.tensor_scalar_max(out=st[:], in0=st[:], scalar1=0.0)
+            else:
+                nc.scalar.activation(out=st[:], in_=yb[g][:], func=AF.Relu, bias=bi[:, 0:1], scale=sc[:, 0:1])
+            nc.sync.dma_start(out=o_v[g], in_=st[:].rearrange("o (b n) -> o b n", b=2))
+            if n < 8:
+                do_mx(2 + n, refill[n])

@@ -56,6 +56,7 @@ def tile_memory_sup_pb_t_kernel(tc, query, concat_memory, conv_w, bn_gamma, bn_b
         mc = {}
         ms = {}
         yb = {}
+        early = {}
 
         guard = const.tile([P, 1], F32, name="guard")
         nc.vector.memset(guard[:], SQRT_GUARD)
@@ -168,8 +169,17 @@ def tile_memory_sup_pb_t_kernel(tc, query, concat_memory, conv_w, bn_gamma, bn_b
             nc.vector.quantize_mx(out=mc[g][:].bitcast(FP8X4), scales=ms[g][:],
                                   in_=gm[g][:].rearrange("p b n j -> p (b n j)"))
 
+        def do_warm(g, src):
+            yb[g] = psum.tile([P, 512], F32, name="yb", tag="y")
+            early[g] = True
+            for rep in range(2):
+                nc.tensor.matmul_mx(out=yb[g][:], lhsT=wc[:, 0:P].bitcast(FP8X4), lhsT_scale=ws[:, 0:P],
+                                    rhs=qc[src][:].bitcast(FP8X4), rhs_scale=qs[src][:], start=True, stop=True)
+
         def do_mx(g, tag):
-            yb[g] = psum.tile([P, 512], F32, name="yb", tag=tag)
+            if not early.get(g, False):
+                yb[g] = psum.tile([P, 512], F32, name="yb", tag=tag)
+            early[g] = False
             nc.tensor.matmul_mx(out=yb[g][:], lhsT=wc[:, 0:P].bitcast(FP8X4), lhsT_scale=ws[:, 0:P],
                                 rhs=qc[g][:].bitcast(FP8X4), rhs_scale=qs[g][:], start=True, stop=False)
             nc.tensor.matmul_mx(out=yb[g][:], lhsT=wc[:, P:2 * P].bitcast(FP8X4), lhsT_scale=ws[:, P:2 * P],
@@ -209,6 +219,8 @@ def tile_memory_sup_pb_t_kernel(tc, query, concat_memory, conv_w, bn_gamma, bn_b
                     if ok(i + 2):
                         do_rc(i + 2)
                         do_rb(i + 2)
+                    if 0 <= i <= 10:
+                        do_warm(i + 1, i)
             if i == -4:
                 prep_w()
             if ok(i + 4):

@@ -17,7 +17,8 @@ FLOPS = 2 * 8192 * 1024 * 128
 
 L2_EPS = 1e-12
 BN_EPS = 1e-5
-SQRT_GUARD = 1e-30
+GW = 64
+HEAD = 2
 
 PINNED = True
 
@@ -35,7 +36,8 @@ def tile_memory_sup_pb_t_kernel(tc, query, concat_memory, conv_w, bn_gamma, bn_b
         keep = ctx.enter_context(tc.tile_pool(name="keep", bufs=1))
         xpool = ctx.enter_context(tc.tile_pool(name="xpool", bufs=7))
         mpool = ctx.enter_context(tc.tile_pool(name="mpool", bufs=4))
-        gqpool = ctx.enter_context(tc.tile_pool(name="gqpool", bufs=2))
+        gqpool = ctx.enter_context(tc.tile_pool(name="gqpool", bufs=1))
+        rpool = ctx.enter_context(tc.tile_pool(name="rpool", bufs=3))
         gmpool = ctx.enter_context(tc.tile_pool(name="gmpool", bufs=3))
         jpool = ctx.enter_context(tc.tile_pool(name="jpool", bufs=2))
         spool = ctx.enter_context(tc.tile_pool(name="spool", bufs=6))
@@ -46,7 +48,7 @@ def tile_memory_sup_pb_t_kernel(tc, query, concat_memory, conv_w, bn_gamma, bn_b
         t1 = {}
         mt = {}
         ss = {}
-        nrm = {}
+        rsb = {}
         rr = {}
         rbk = {}
         gq = {}
@@ -56,14 +58,13 @@ def tile_memory_sup_pb_t_kernel(tc, query, concat_memory, conv_w, bn_gamma, bn_b
         mc = {}
         ms = {}
         yb = {}
-        early = {}
 
-        guard = const.tile([P, 1], F32, name="guard")
-        nc.vector.memset(guard[:], SQRT_GUARD)
-        bneps = const.tile([P, 1], F32, name="bneps")
-        nc.vector.memset(bneps[:], BN_EPS)
+        one = const.tile([P, 1], F32, name="one")
+        nc.vector.memset(one[:], 1.0)
+        mhalf = const.tile([P, 4], F32, name="mhalf")
+        nc.vector.memset(mhalf[:], -0.5)
         warm = const.tile([P, 1], F32, name="warm")
-        nc.scalar.activation(out=warm[:], in_=bneps[:], func=AF.Sqrt)
+        nc.scalar.activation(out=warm[:], in_=one[:], func=AF.Square)
         ident = const.tile([P, P], F32, name="ident")
         make_identity(nc, ident[:])
         gam_b = const.tile([P, 1], BF16, name="gam_b")
@@ -115,15 +116,16 @@ def tile_memory_sup_pb_t_kernel(tc, query, concat_memory, conv_w, bn_gamma, bn_b
                 nc.scalar.activation(out=junk[:], in_=tb[:, :, :, e], func=AF.Square,
                                      accum_out=ss[g][:, 2 * b + e:2 * b + e + 1])
 
-        def do_sqrt(g):
-            nrm[g] = spool.tile([P, 4], F32, name="nrm")
-            nc.scalar.activation(out=nrm[g][:], in_=ss[g][:], func=AF.Sqrt, bias=guard[:, 0:1])
-
-        def do_rc(g):
-            rm = spool.tile([P, 4], F32, name="rm")
-            nc.vector.tensor_scalar_max(out=rm[:], in0=nrm[g][:], scalar1=L2_EPS)
+        def do_pow(g):
+            cl = spool.tile([P, 4], F32, name="cl")
+            nc.gpsimd.tensor_scalar(out=cl[:], in0=ss[g][:], scalar1=3.0e38, scalar2=L2_EPS * L2_EPS,
+                                    op0=ALU.min, op1=ALU.max)
             rr[g] = spool.tile([P, 4], F32, name="rr")
-            nc.vector.reciprocal(out=rr[g][:], in_=rm[:])
+            nc.gpsimd.tensor_tensor(out=rr[g][:], in0=cl[:], in1=mhalf[:], op=ALU.pow)
+
+        def do_rsb(g):
+            rsb[g] = rpool.tile([P, GW, 2], F32, name="rsb")
+            nc.scalar.copy(out=rsb[g][:], in_=rbk[g][:, 1, :, P - GW:P].rearrange("p e w -> p w e"))
 
         def do_rb(g):
             rbk[g] = psum.tile([P, 2, 2, P], F32, name="rbk", tag="rb")
@@ -132,13 +134,21 @@ def tile_memory_sup_pb_t_kernel(tc, query, concat_memory, conv_w, bn_gamma, bn_b
                     c = 2 * b + e
                     nc.tensor.transpose(rbk[g][:, b, e, :], rr[g][:, c:c + 1].to_broadcast([P, P]), ident[:])
 
+        def do_bmg(g):
+            gq[g] = gqpool.tile([P, 2, 256, 4], BF16, name="gq", align_bytes=64)
+            nc.gpsimd.tensor_tensor(
+                out=gq[g][:, 1, 2 * (P - GW):256, :],
+                in0=xq[g][:, 1, :, 2 * (P - GW):256].rearrange("p j n -> p n j"),
+                in1=rsb[g][:].rearrange("p w e -> p (w e)").unsqueeze(2).to_broadcast([P, 2 * GW, 4]),
+                op=ALU.mult,
+            )
+
         def do_bm(g, b):
-            if b == 0:
-                gq[g] = gqpool.tile([P, 2, 256, 4], BF16, name="gq", align_bytes=64)
+            nw = P if b == 0 else P - GW
             nc.vector.tensor_tensor(
-                out=gq[g][:, b].rearrange("p (w e) j -> p w e j", e=2),
-                in0=xq[g][:, b].rearrange("p j (w e) -> p w e j", e=2),
-                in1=rbk[g][:, b].rearrange("p e w -> p w e").unsqueeze(3).to_broadcast([P, P, 2, 4]),
+                out=gq[g][:, b, 0:2 * nw, :].rearrange("p (w e) j -> p w e j", e=2),
+                in0=xq[g][:, b, :, 0:2 * nw].rearrange("p j (w e) -> p w e j", e=2),
+                in1=rbk[g][:, b, :, 0:nw].rearrange("p e w -> p w e").unsqueeze(3).to_broadcast([P, nw, 2, 4]),
                 op=ALU.mult,
             )
 
@@ -158,10 +168,12 @@ def tile_memory_sup_pb_t_kernel(tc, query, concat_memory, conv_w, bn_gamma, bn_b
         def do_me(g, b):
             if b == 0:
                 gm[g] = gmpool.tile([P, 2, 256, 4], BF16, name="gm", align_bytes=64)
-            nc.scalar.copy(
-                out=gm[g][:].bitcast(F32)[:, b].rearrange("p (r t) u -> p r t u", t=2),
-                in_=mt[(g, b)][:].rearrange("p u t r -> p r t u"),
-            )
+            dst = gm[g][:].bitcast(F32)[:, b].rearrange("p (r t) u -> p r t u", t=2)
+            src = mt[(g, b)][:].rearrange("p u t r -> p r t u")
+            if g < HEAD:
+                nc.vector.tensor_copy(out=dst, in_=src)
+            else:
+                nc.scalar.copy(out=dst, in_=src)
 
         def do_qm(g):
             mc[g] = keep.tile([P, 512], U32, name="mc%d" % g, align_bytes=64)
@@ -169,17 +181,8 @@ def tile_memory_sup_pb_t_kernel(tc, query, concat_memory, conv_w, bn_gamma, bn_b
             nc.vector.quantize_mx(out=mc[g][:].bitcast(FP8X4), scales=ms[g][:],
                                   in_=gm[g][:].rearrange("p b n j -> p (b n j)"))
 
-        def do_warm(g, src):
-            yb[g] = psum.tile([P, 512], F32, name="yb", tag="y")
-            early[g] = True
-            for rep in range(2):
-                nc.tensor.matmul_mx(out=yb[g][:], lhsT=wc[:, 0:P].bitcast(FP8X4), lhsT_scale=ws[:, 0:P],
-                                    rhs=qc[src][:].bitcast(FP8X4), rhs_scale=qs[src][:], start=True, stop=True)
-
         def do_mx(g, tag):
-            if not early.get(g, False):
-                yb[g] = psum.tile([P, 512], F32, name="yb", tag=tag)
-            early[g] = False
+            yb[g] = psum.tile([P, 512], F32, name="yb", tag=tag)
             nc.tensor.matmul_mx(out=yb[g][:], lhsT=wc[:, 0:P].bitcast(FP8X4), lhsT_scale=ws[:, 0:P],
                                 rhs=qc[g][:].bitcast(FP8X4), rhs_scale=qs[g][:], start=True, stop=False)
             nc.tensor.matmul_mx(out=yb[g][:], lhsT=wc[:, P:2 * P].bitcast(FP8X4), lhsT_scale=ws[:, P:2 * P],
@@ -206,6 +209,12 @@ def tile_memory_sup_pb_t_kernel(tc, query, concat_memory, conv_w, bn_gamma, bn_b
                 do_mx(0, "rb")
             if i == 15:
                 do_mx(1, "rb")
+            if ok(i + 2):
+                do_rb(i + 2)
+            if ok(i + 1):
+                do_bmg(i + 1)
+            if ok(i + 3):
+                do_pow(i + 3)
             for b in range(2):
                 if ok(i + 4):
                     do_t1(i + 4, b)
@@ -215,16 +224,10 @@ def tile_memory_sup_pb_t_kernel(tc, query, concat_memory, conv_w, bn_gamma, bn_b
                     do_me(i + 3, b)
                 if ok(i + 1):
                     do_bm(i + 1, b)
-                if b == 0:
-                    if ok(i + 2):
-                        do_rc(i + 2)
-                        do_rb(i + 2)
-                    if 0 <= i <= 10:
-                        do_warm(i + 1, i)
+            if ok(i + 2):
+                do_rsb(i + 2)
             if i == -4:
                 prep_w()
-            if ok(i + 4):
-                do_sqrt(i + 4)
             if ok(i):
                 do_bs(i)
             if i == 2:
@@ -237,10 +240,10 @@ def tile_memory_sup_pb_t_kernel(tc, query, concat_memory, conv_w, bn_gamma, bn_b
 
         mv = const.tile([P, 2], F32, name="mv")
         nc.vector.bn_aggr(out=mv[:], in_=stats[:].rearrange("p g s -> p (g s)"))
-        sd = const.tile([P, 1], F32, name="sd")
-        nc.scalar.activation(out=sd[:], in_=mv[:, 1:2], func=AF.Sqrt, bias=bneps[:, 0:1])
         rs = const.tile([P, 1], F32, name="rs")
-        nc.vector.reciprocal(out=rs[:], in_=sd[:])
+        ve = const.tile([P, 1], F32, name="ve")
+        nc.gpsimd.tensor_scalar(out=ve[:], in0=mv[:, 1:2], scalar1=BN_EPS, scalar2=1.0, op0=ALU.add, op1=ALU.mult)
+        nc.gpsimd.tensor_tensor(out=rs[:], in0=ve[:], in1=mhalf[:, 0:1], op=ALU.pow)
         sc = const.tile([P, 1], F32, name="sc")
         nc.vector.tensor_tensor(out=sc[:], in0=rs[:], in1=gam[:], op=ALU.mult)
         nb = const.tile([P, 1], F32, name="nb")

@@ -17,8 +17,6 @@ FLOPS = 2 * 8192 * 1024 * 128
 
 L2_EPS = 1e-12
 BN_EPS = 1e-5
-GW = 64
-HEAD = 2
 
 PINNED = True
 
@@ -36,9 +34,8 @@ def tile_memory_sup_pb_t_kernel(tc, query, concat_memory, conv_w, bn_gamma, bn_b
         keep = ctx.enter_context(tc.tile_pool(name="keep", bufs=1))
         xpool = ctx.enter_context(tc.tile_pool(name="xpool", bufs=7))
         mpool = ctx.enter_context(tc.tile_pool(name="mpool", bufs=4))
-        gqpool = ctx.enter_context(tc.tile_pool(name="gqpool", bufs=1))
-        rpool = ctx.enter_context(tc.tile_pool(name="rpool", bufs=3))
-        gmpool = ctx.enter_context(tc.tile_pool(name="gmpool", bufs=3))
+        gqpool = ctx.enter_context(tc.tile_pool(name="gqpool", bufs=2))
+        gmpool = ctx.enter_context(tc.tile_pool(name="gmpool", bufs=4))
         jpool = ctx.enter_context(tc.tile_pool(name="jpool", bufs=2))
         spool = ctx.enter_context(tc.tile_pool(name="spool", bufs=6))
         psum = ctx.enter_context(tc.psum_pool(name="psum", bufs=2))
@@ -48,7 +45,7 @@ def tile_memory_sup_pb_t_kernel(tc, query, concat_memory, conv_w, bn_gamma, bn_b
         t1 = {}
         mt = {}
         ss = {}
-        rsb = {}
+        rq = {}
         rr = {}
         rbk = {}
         gq = {}
@@ -61,10 +58,8 @@ def tile_memory_sup_pb_t_kernel(tc, query, concat_memory, conv_w, bn_gamma, bn_b
 
         one = const.tile([P, 1], F32, name="one")
         nc.vector.memset(one[:], 1.0)
-        mhalf = const.tile([P, 4], F32, name="mhalf")
-        nc.vector.memset(mhalf[:], -0.5)
         warm = const.tile([P, 1], F32, name="warm")
-        nc.scalar.activation(out=warm[:], in_=one[:], func=AF.Square)
+        nc.scalar.activation(out=warm[:], in_=one[:], func=AF.Abs_reciprocal_sqrt)
         ident = const.tile([P, P], F32, name="ident")
         make_identity(nc, ident[:])
         gam_b = const.tile([P, 1], BF16, name="gam_b")
@@ -91,13 +86,16 @@ def tile_memory_sup_pb_t_kernel(tc, query, concat_memory, conv_w, bn_gamma, bn_b
         def load_w():
             nc.sync.dma_start(out=wsb[:], in_=conv_w)
 
-        def prep_w():
+        wps = psum.tile([P, 4, P], F32, name="wps", tag="y")
+
+        def turn_w():
             w32 = wsb[:].bitcast(F32)
-            wps = psum.tile([P, 4, P], F32, name="wps", tag="y")
             for h in range(2):
                 nc.tensor.transpose(wps[:, h, :], w32[:, h:256:2], ident[:])
             for u in range(2):
                 nc.tensor.transpose(wps[:, 2 + u, :], w32[:, 256 + P * u:256 + P * u + P], ident[:])
+
+        def quant_w():
             nc.vector.tensor_copy(out=gw[:].bitcast(F32), in_=wps[:].rearrange("p (a h) o -> p a o h", a=2))
             nc.vector.quantize_mx(out=wc[:].bitcast(FP8X4), scales=ws[:], in_=gw[:].rearrange("p a o t -> p (a o t)"))
 
@@ -116,39 +114,28 @@ def tile_memory_sup_pb_t_kernel(tc, query, concat_memory, conv_w, bn_gamma, bn_b
                 nc.scalar.activation(out=junk[:], in_=tb[:, :, :, e], func=AF.Square,
                                      accum_out=ss[g][:, 2 * b + e:2 * b + e + 1])
 
-        def do_pow(g):
-            cl = spool.tile([P, 4], F32, name="cl")
-            nc.gpsimd.tensor_scalar(out=cl[:], in0=ss[g][:], scalar1=3.0e38, scalar2=L2_EPS * L2_EPS,
-                                    op0=ALU.min, op1=ALU.max)
-            rr[g] = spool.tile([P, 4], F32, name="rr")
-            nc.gpsimd.tensor_tensor(out=rr[g][:], in0=cl[:], in1=mhalf[:], op=ALU.pow)
+        def do_rsq(g):
+            rq[g] = spool.tile([P, 4], F32, name="rq")
+            nc.scalar.activation(out=rq[g][:], in_=ss[g][:], func=AF.Abs_reciprocal_sqrt)
 
-        def do_rsb(g):
-            rsb[g] = rpool.tile([P, GW, 2], F32, name="rsb")
-            nc.scalar.copy(out=rsb[g][:], in_=rbk[g][:, 1, :, P - GW:P].rearrange("p e w -> p w e"))
+        def do_rc(g):
+            rr[g] = spool.tile([P, 4], F32, name="rr")
+            nc.gpsimd.tensor_scalar(out=rr[g][:], in0=rq[g][:], scalar1=1.0 / L2_EPS, scalar2=0.0,
+                                    op0=ALU.min, op1=ALU.max)
 
         def do_rb(g):
             rbk[g] = psum.tile([P, 2, 2, P], F32, name="rbk", tag="rb")
             for b in range(2):
                 for e in range(2):
                     c = 2 * b + e
-                    nc.tensor.transpose(rbk[g][:, b, e, :], rr[g][:, c:c + 1].to_broadcast([P, P]), ident[:])
+                    nc.tensor.transpose(rbk[g][:, e, b, :], rr[g][:, c:c + 1].to_broadcast([P, P]), ident[:])
 
-        def do_bmg(g):
+        def do_bm(g):
             gq[g] = gqpool.tile([P, 2, 256, 4], BF16, name="gq", align_bytes=64)
-            nc.gpsimd.tensor_tensor(
-                out=gq[g][:, 1, 2 * (P - GW):256, :],
-                in0=xq[g][:, 1, :, 2 * (P - GW):256].rearrange("p j n -> p n j"),
-                in1=rsb[g][:].rearrange("p w e -> p (w e)").unsqueeze(2).to_broadcast([P, 2 * GW, 4]),
-                op=ALU.mult,
-            )
-
-        def do_bm(g, b):
-            nw = P if b == 0 else P - GW
             nc.vector.tensor_tensor(
-                out=gq[g][:, b, 0:2 * nw, :].rearrange("p (w e) j -> p w e j", e=2),
-                in0=xq[g][:, b, :, 0:2 * nw].rearrange("p j (w e) -> p w e j", e=2),
-                in1=rbk[g][:, b, :, 0:nw].rearrange("p e w -> p w e").unsqueeze(3).to_broadcast([P, nw, 2, 4]),
+                out=gq[g][:].rearrange("p b (w e) j -> p b w e j", e=2),
+                in0=xq[g][:].rearrange("p b j (w e) -> p b w e j", e=2),
+                in1=rbk[g][:].rearrange("p e b w -> p b w e").unsqueeze(4).to_broadcast([P, 2, P, 2, 4]),
                 op=ALU.mult,
             )
 
@@ -168,12 +155,10 @@ def tile_memory_sup_pb_t_kernel(tc, query, concat_memory, conv_w, bn_gamma, bn_b
         def do_me(g, b):
             if b == 0:
                 gm[g] = gmpool.tile([P, 2, 256, 4], BF16, name="gm", align_bytes=64)
-            dst = gm[g][:].bitcast(F32)[:, b].rearrange("p (r t) u -> p r t u", t=2)
-            src = mt[(g, b)][:].rearrange("p u t r -> p r t u")
-            if g < HEAD:
-                nc.vector.tensor_copy(out=dst, in_=src)
-            else:
-                nc.scalar.copy(out=dst, in_=src)
+            nc.scalar.copy(
+                out=gm[g][:].bitcast(F32)[:, b].rearrange("p (r t) u -> p r t u", t=2),
+                in_=mt[(g, b)][:].rearrange("p u t r -> p r t u"),
+            )
 
         def do_qm(g):
             mc[g] = keep.tile([P, 512], U32, name="mc%d" % g, align_bytes=64)
@@ -196,25 +181,25 @@ def tile_memory_sup_pb_t_kernel(tc, query, concat_memory, conv_w, bn_gamma, bn_b
 
         first_tag = {12: "t1", 13: "t1", 14: "mt", 15: "mt"}
 
-        for i in range(-7, NG):
+        for i in range(-7, NG + 1):
             if ok(i + 6):
                 load_m(i + 6)
-            if i == -6:
-                load_w()
             if ok(i + 7):
                 load_x(i + 7)
-            if ok(i):
-                do_mx(i, first_tag.get(i, "y"))
-            if i == 14:
-                do_mx(0, "rb")
-            if i == 15:
-                do_mx(1, "rb")
+            if i == -6:
+                load_w()
             if ok(i + 2):
                 do_rb(i + 2)
+            if i == -2:
+                turn_w()
+            if ok(i - 1):
+                do_mx(i - 1, first_tag.get(i - 1, "y"))
+            if i == 15:
+                do_mx(0, "rb")
+            if i == 16:
+                do_mx(1, "rb")
             if ok(i + 1):
-                do_bmg(i + 1)
-            if ok(i + 3):
-                do_pow(i + 3)
+                do_bm(i + 1)
             for b in range(2):
                 if ok(i + 4):
                     do_t1(i + 4, b)
@@ -222,28 +207,26 @@ def tile_memory_sup_pb_t_kernel(tc, query, concat_memory, conv_w, bn_gamma, bn_b
                 if ok(i + 3):
                     do_m1(i + 3, b)
                     do_me(i + 3, b)
-                if ok(i + 1):
-                    do_bm(i + 1, b)
-            if ok(i + 2):
-                do_rsb(i + 2)
-            if i == -4:
-                prep_w()
-            if ok(i):
-                do_bs(i)
+            if ok(i + 4):
+                do_rsq(i + 4)
+                do_rc(i + 4)
+            if i == -1:
+                quant_w()
+            if ok(i - 1):
+                do_bs(i - 1)
             if i == 2:
                 nc.vector.tensor_copy(out=gam[:], in_=gam_b[:])
                 nc.vector.tensor_copy(out=bet[:], in_=bet_b[:])
-            if ok(i + 2):
-                do_qm(i + 2)
             if ok(i + 1):
+                do_qm(i + 1)
                 do_qq(i + 1)
 
         mv = const.tile([P, 2], F32, name="mv")
         nc.vector.bn_aggr(out=mv[:], in_=stats[:].rearrange("p g s -> p (g s)"))
         rs = const.tile([P, 1], F32, name="rs")
         ve = const.tile([P, 1], F32, name="ve")
-        nc.gpsimd.tensor_scalar(out=ve[:], in0=mv[:, 1:2], scalar1=BN_EPS, scalar2=1.0, op0=ALU.add, op1=ALU.mult)
-        nc.gpsimd.tensor_tensor(out=rs[:], in0=ve[:], in1=mhalf[:, 0:1], op=ALU.pow)
+        nc.vector.tensor_scalar_add(out=ve[:], in0=mv[:, 1:2], scalar1=BN_EPS)
+        nc.scalar.activation(out=rs[:], in_=ve[:], func=AF.Abs_reciprocal_sqrt)
         sc = const.tile([P, 1], F32, name="sc")
         nc.vector.tensor_tensor(out=sc[:], in0=rs[:], in1=gam[:], op=ALU.mult)
         nb = const.tile([P, 1], F32, name="nb")

@@ -55,6 +55,7 @@ def tile_memory_sup_pb_t_kernel(tc, query, concat_memory, conv_w, bn_gamma, bn_b
         mc = {}
         ms = {}
         yb = {}
+        early = {}
 
         one = const.tile([P, 1], F32, name="one")
         nc.vector.memset(one[:], 1.0)
@@ -166,8 +167,17 @@ def tile_memory_sup_pb_t_kernel(tc, query, concat_memory, conv_w, bn_gamma, bn_b
             nc.vector.quantize_mx(out=mc[g][:].bitcast(FP8X4), scales=ms[g][:],
                                   in_=gm[g][:].rearrange("p b n j -> p (b n j)"))
 
+        def do_warm(g, src):
+            yb[g] = psum.tile([P, 512], F32, name="yb", tag="y")
+            early[g] = True
+            for rep in range(2):
+                nc.tensor.matmul_mx(out=yb[g][:], lhsT=wc[:, 0:P].bitcast(FP8X4), lhsT_scale=ws[:, 0:P],
+                                    rhs=qc[src][:].bitcast(FP8X4), rhs_scale=qs[src][:], start=True, stop=True)
+
         def do_mx(g, tag):
-            yb[g] = psum.tile([P, 512], F32, name="yb", tag=tag)
+            if not early.get(g, False):
+                yb[g] = psum.tile([P, 512], F32, name="yb", tag=tag)
+            early[g] = False
             nc.tensor.matmul_mx(out=yb[g][:], lhsT=wc[:, 0:P].bitcast(FP8X4), lhsT_scale=ws[:, 0:P],
                                 rhs=qc[g][:].bitcast(FP8X4), rhs_scale=qs[g][:], start=True, stop=False)
             nc.tensor.matmul_mx(out=yb[g][:], lhsT=wc[:, P:2 * P].bitcast(FP8X4), lhsT_scale=ws[:, P:2 * P],
@@ -207,6 +217,8 @@ def tile_memory_sup_pb_t_kernel(tc, query, concat_memory, conv_w, bn_gamma, bn_b
                 if ok(i + 3):
                     do_m1(i + 3, b)
                     do_me(i + 3, b)
+                if b == 0 and 1 <= i <= 11:
+                    do_warm(i, i - 1)
             if ok(i + 4):
                 do_rsq(i + 4)
                 do_rc(i + 4)

@@ -19,6 +19,8 @@ L2_EPS = 1e-12
 BN_EPS = 1e-5
 
 PINNED = True
+LATE = [11, 12, 13, 14]
+NV = NG - len(LATE)
 
 
 def tile_memory_sup_pb_t_kernel(tc, query, concat_memory, conv_w, bn_gamma, bn_beta, out):
@@ -55,7 +57,6 @@ def tile_memory_sup_pb_t_kernel(tc, query, concat_memory, conv_w, bn_gamma, bn_b
         mc = {}
         ms = {}
         yb = {}
-        early = {}
 
         one = const.tile([P, 1], F32, name="one")
         nc.vector.memset(one[:], 1.0)
@@ -70,7 +71,11 @@ def tile_memory_sup_pb_t_kernel(tc, query, concat_memory, conv_w, bn_gamma, bn_b
             nc.gpsimd.dma_start(out=bet_b[:], in_=bn_beta.rearrange("(o one) -> o one", one=1))
         gam = const.tile([P, 1], F32, name="gam")
         bet = const.tile([P, 1], F32, name="bet")
-        stats = const.tile([P, NG, 6], F32, name="stats")
+        stats = const.tile([P, 6 * NV + 3 * len(LATE)], F32, name="stats")
+        late = stats[:, 6 * NV:].rearrange("p (k s) -> p k s", s=3)
+        nc.vector.memset(late, 512.0)
+        sums = const.tile([P, len(LATE)], F32, name="sums")
+        negm = const.tile([P, len(LATE)], F32, name="negm")
         wsb = const.tile([P, 1024], BF16, name="wsb")
         gw = const.tile([P, 2, P, 4], BF16, name="gw", align_bytes=64)
         wc = const.tile([P, 2 * P], U32, name="wc", align_bytes=64)
@@ -78,7 +83,12 @@ def tile_memory_sup_pb_t_kernel(tc, query, concat_memory, conv_w, bn_gamma, bn_b
 
         def load_x(g):
             xq[g] = xpool.tile([P, 2, 4, 256], BF16, name="xq")
-            nc.sync.dma_start(out=xq[g][:].rearrange("p b j n -> p b (j n)"), in_=q_v[g])
+            dst = xq[g][:].rearrange("p b j n -> p b (j n)")
+            if g == 0:
+                for b in range(2):
+                    nc.sync.dma_start(out=dst[:, b], in_=q_v[g][:, b])
+            else:
+                nc.sync.dma_start(out=dst, in_=q_v[g])
 
         def load_m(g):
             mm[g] = mpool.tile([P, 2, 2, 512], BF16, name="mm")
@@ -167,24 +177,26 @@ def tile_memory_sup_pb_t_kernel(tc, query, concat_memory, conv_w, bn_gamma, bn_b
             nc.vector.quantize_mx(out=mc[g][:].bitcast(FP8X4), scales=ms[g][:],
                                   in_=gm[g][:].rearrange("p b n j -> p (b n j)"))
 
-        def do_warm(g, src):
-            yb[g] = psum.tile([P, 512], F32, name="yb", tag="y")
-            early[g] = True
-            for rep in range(2):
-                nc.tensor.matmul_mx(out=yb[g][:], lhsT=wc[:, 0:P].bitcast(FP8X4), lhsT_scale=ws[:, 0:P],
-                                    rhs=qc[src][:].bitcast(FP8X4), rhs_scale=qs[src][:], start=True, stop=True)
-
         def do_mx(g, tag):
-            if not early.get(g, False):
-                yb[g] = psum.tile([P, 512], F32, name="yb", tag=tag)
-            early[g] = False
+            yb[g] = psum.tile([P, 512], F32, name="yb", tag=tag)
             nc.tensor.matmul_mx(out=yb[g][:], lhsT=wc[:, 0:P].bitcast(FP8X4), lhsT_scale=ws[:, 0:P],
                                 rhs=qc[g][:].bitcast(FP8X4), rhs_scale=qs[g][:], start=True, stop=False)
             nc.tensor.matmul_mx(out=yb[g][:], lhsT=wc[:, P:2 * P].bitcast(FP8X4), lhsT_scale=ws[:, P:2 * P],
                                 rhs=mc[g][:].bitcast(FP8X4), rhs_scale=ms[g][:], start=False, stop=True)
 
         def do_bs(g):
-            nc.vector.bn_stats(out=stats[:, g, :], in_=yb[g][:])
+            if g in LATE:
+                k = LATE.index(g)
+                junk = jpool.tile([P, 512], BF16, name="junk")
+                nc.scalar.activation(out=junk[:], in_=yb[g][:], func=AF.Identity, accum_out=sums[:, k:k + 1])
+                nc.scalar.mul(out=late[:, k, 1:2], in_=sums[:, k:k + 1], mul=1.0 / 512.0)
+                nc.scalar.mul(out=negm[:, k:k + 1], in_=sums[:, k:k + 1], mul=-1.0 / 512.0)
+                junk = jpool.tile([P, 512], BF16, name="junk")
+                nc.scalar.activation(out=junk[:], in_=yb[g][:], func=AF.Square, bias=negm[:, k:k + 1],
+                                     accum_out=late[:, k, 2:3])
+            else:
+                s = g if g < LATE[0] else g - len(LATE)
+                nc.vector.bn_stats(out=stats[:, 6 * s:6 * s + 6], in_=yb[g][:])
 
         def ok(g):
             return 0 <= g < NG
@@ -196,12 +208,10 @@ def tile_memory_sup_pb_t_kernel(tc, query, concat_memory, conv_w, bn_gamma, bn_b
                 load_m(i + 6)
             if ok(i + 7):
                 load_x(i + 7)
-            if i == -6:
+            if i == -7:
                 load_w()
-            if ok(i + 2):
+            if i > -2 and ok(i + 2):
                 do_rb(i + 2)
-            if i == -2:
-                turn_w()
             if ok(i - 1):
                 do_mx(i - 1, first_tag.get(i - 1, "y"))
             if i == 15:
@@ -217,13 +227,14 @@ def tile_memory_sup_pb_t_kernel(tc, query, concat_memory, conv_w, bn_gamma, bn_b
                 if ok(i + 3):
                     do_m1(i + 3, b)
                     do_me(i + 3, b)
-                if b == 0 and 1 <= i <= 11:
-                    do_warm(i, i - 1)
+                if i == -3 and b == 0:
+                    do_rb(0)
+            if i == -4:
+                turn_w()
+                quant_w()
             if ok(i + 4):
                 do_rsq(i + 4)
                 do_rc(i + 4)
-            if i == -1:
-                quant_w()
             if ok(i - 1):
                 do_bs(i - 1)
             if i == 2:
@@ -234,18 +245,15 @@ def tile_memory_sup_pb_t_kernel(tc, query, concat_memory, conv_w, bn_gamma, bn_b
                 do_qq(i + 1)
 
         mv = const.tile([P, 2], F32, name="mv")
-        nc.vector.bn_aggr(out=mv[:], in_=stats[:].rearrange("p g s -> p (g s)"))
+        nc.vector.bn_aggr(out=mv[:], in_=stats[:])
+        nmean = const.tile([P, 1], F32, name="nmean")
+        nc.vector.tensor_scalar_mul(out=nmean[:], in0=mv[:, 0:1], scalar1=-1.0)
         rs = const.tile([P, 1], F32, name="rs")
-        ve = const.tile([P, 1], F32, name="ve")
-        nc.vector.tensor_scalar_add(out=ve[:], in0=mv[:, 1:2], scalar1=BN_EPS)
-        nc.scalar.activation(out=rs[:], in_=ve[:], func=AF.Abs_reciprocal_sqrt)
+        nc.scalar.activation(out=rs[:], in_=mv[:, 1:2], func=AF.Abs_reciprocal_sqrt, bias=BN_EPS)
         sc = const.tile([P, 1], F32, name="sc")
-        nc.vector.tensor_tensor(out=sc[:], in0=rs[:], in1=gam[:], op=ALU.mult)
-        nb = const.tile([P, 1], F32, name="nb")
-        nc.vector.tensor_scalar(out=nb[:], in0=mv[:, 0:1], scalar1=sc[:, 0:1], scalar2=-1.0,
-                                op0=ALU.mult, op1=ALU.mult)
+        nc.scalar.mul(out=sc[:], in_=rs[:], mul=gam[:, 0:1])
         bi = const.tile([P, 1], F32, name="bi")
-        nc.vector.tensor_tensor(out=bi[:], in0=nb[:], in1=bet[:], op=ALU.add)
+        nc.scalar.activation(out=bi[:], in_=sc[:], func=AF.Identity, bias=bet[:, 0:1], scale=nmean[:, 0:1])
 
         order = [10, 11, 12, 13, 14, 15, 0, 1, 2, 3, 4, 5, 6, 7, 8, 9]
         refill = ["y", "y", "t1", "t1", "mt", "mt", "rb", "rb"]

@@ -19,7 +19,7 @@ L2_EPS = 1e-12
 BN_EPS = 1e-5
 
 PINNED = True
-LATE = [11, 12, 13, 14]
+LATE = [10, 11, 12, 13]
 NV = NG - len(LATE)
 
 
@@ -235,14 +235,14 @@ def tile_memory_sup_pb_t_kernel(tc, query, concat_memory, conv_w, bn_gamma, bn_b
             if ok(i + 4):
                 do_rsq(i + 4)
                 do_rc(i + 4)
-            if ok(i - 1):
-                do_bs(i - 1)
             if i == 2:
                 nc.vector.tensor_copy(out=gam[:], in_=gam_b[:])
                 nc.vector.tensor_copy(out=bet[:], in_=bet_b[:])
             if ok(i + 1):
                 do_qm(i + 1)
                 do_qq(i + 1)
+            if ok(i - 1):
+                do_bs(i - 1)
 
         mv = const.tile([P, 2], F32, name="mv")
         nc.vector.bn_aggr(out=mv[:], in_=stats[:])

@@ -12,51 +12,62 @@ AF = mybir.ActivationFunctionType
 ALU = mybir.AluOpType
 
 P = 128
-NG = 16
+PACK = 4
+GROUPS = 16
+IMAGES = 2
+PIXELS = 256
+GROUP_PIXELS = IMAGES * PIXELS
 FLOPS = 2 * 8192 * 1024 * 128
 
 L2_EPS = 1e-12
 BN_EPS = 1e-5
 
-PINNED = True
-LATE = [10, 11, 12, 13]
-NV = NG - len(LATE)
+LOAD_QUERY_AHEAD = 7
+LOAD_MEMORY_AHEAD = 6
+SQUARE_AHEAD = 4
+MEMORY_AHEAD = 3
+SPREAD_AHEAD = 2
+QUANTISE_AHEAD = 1
+MX_BEHIND = 1
+
+SCALAR_STATS = [10, 11, 12, 13]
+VECTOR_STATS = GROUPS - len(SCALAR_STATS)
 
 
 def tile_memory_sup_pb_t_kernel(tc, query, concat_memory, conv_w, bn_gamma, bn_beta, out):
     nc = tc.nc
-    q_v = query.rearrange("(g b) (p j) h w -> g p b (j h w)", b=2, j=4)
-    m_v = concat_memory.rearrange("(g b p t) k -> g p b (t k)", b=2, p=P, t=2)
-    o_v = out.rearrange("(g b) o h w -> g o b (h w)", b=2)
+    query_view = query.rearrange("(g b) (p j) h w -> g p b (j h w)", b=IMAGES, j=PACK)
+    memory_view = concat_memory.rearrange("(g b p t) k -> g p b (t k)", b=IMAGES, p=P, t=2)
+    out_view = out.rearrange("(g b) o h w -> g o b (h w)", b=IMAGES)
 
     with ExitStack() as ctx:
-        if PINNED:
-            ctx.enter_context(tc.manual_schedule())
+        ctx.enter_context(tc.manual_schedule())
         const = ctx.enter_context(tc.tile_pool(name="const", bufs=1))
         keep = ctx.enter_context(tc.tile_pool(name="keep", bufs=1))
-        xpool = ctx.enter_context(tc.tile_pool(name="xpool", bufs=7))
-        mpool = ctx.enter_context(tc.tile_pool(name="mpool", bufs=4))
-        gqpool = ctx.enter_context(tc.tile_pool(name="gqpool", bufs=2))
-        gmpool = ctx.enter_context(tc.tile_pool(name="gmpool", bufs=4))
-        jpool = ctx.enter_context(tc.tile_pool(name="jpool", bufs=2))
-        spool = ctx.enter_context(tc.tile_pool(name="spool", bufs=6))
+        query_pool = ctx.enter_context(tc.tile_pool(name="query_pool", bufs=LOAD_QUERY_AHEAD - QUANTISE_AHEAD + 1))
+        memory_pool = ctx.enter_context(tc.tile_pool(name="memory_pool", bufs=LOAD_MEMORY_AHEAD - MEMORY_AHEAD + 1))
+        norm_pool = ctx.enter_context(tc.tile_pool(name="norm_pool", bufs=SQUARE_AHEAD - SPREAD_AHEAD + 1))
+        m_pool = ctx.enter_context(tc.tile_pool(name="m_pool", bufs=MEMORY_AHEAD - QUANTISE_AHEAD + 2))
+        q_pool = ctx.enter_context(tc.tile_pool(name="q_pool", bufs=2))
+        unread_pool = ctx.enter_context(tc.tile_pool(name="unread_pool", bufs=2))
         psum = ctx.enter_context(tc.psum_pool(name="psum", bufs=2))
 
-        xq = {}
-        mm = {}
-        t1 = {}
-        mt = {}
-        ss = {}
-        rq = {}
-        rr = {}
-        rbk = {}
-        gq = {}
-        gm = {}
-        qc = {}
-        qs = {}
-        mc = {}
-        ms = {}
-        yb = {}
+        query_tile = {}
+        memory_tile = {}
+        turned_q = {}
+        turned_m = {}
+        squares = {}
+        inv_raw = {}
+        inv_norm = {}
+        spread = {}
+        q_grouped = {}
+        m_grouped = {}
+        q_codes = {}
+        q_scales = {}
+        m_codes = {}
+        m_scales = {}
+        sums = {}
+        bank_of = {}
 
         one = const.tile([P, 1], F32, name="one")
         nc.vector.memset(one[:], 1.0)
@@ -64,207 +75,202 @@ def tile_memory_sup_pb_t_kernel(tc, query, concat_memory, conv_w, bn_gamma, bn_b
         nc.scalar.activation(out=warm[:], in_=one[:], func=AF.Abs_reciprocal_sqrt)
         ident = const.tile([P, P], F32, name="ident")
         make_identity(nc, ident[:])
-        gam_b = const.tile([P, 1], BF16, name="gam_b")
-        bet_b = const.tile([P, 1], BF16, name="bet_b")
+        gamma = const.tile([P, 1], BF16, name="gamma")
+        beta = const.tile([P, 1], BF16, name="beta")
         with nc.allow_non_contiguous_dma(reason="one bn parameter per partition"):
-            nc.gpsimd.dma_start(out=gam_b[:], in_=bn_gamma.rearrange("(o one) -> o one", one=1))
-            nc.gpsimd.dma_start(out=bet_b[:], in_=bn_beta.rearrange("(o one) -> o one", one=1))
-        gam = const.tile([P, 1], F32, name="gam")
-        bet = const.tile([P, 1], F32, name="bet")
-        stats = const.tile([P, 6 * NV + 3 * len(LATE)], F32, name="stats")
-        late = stats[:, 6 * NV:].rearrange("p (k s) -> p k s", s=3)
-        nc.vector.memset(late, 512.0)
-        sums = const.tile([P, len(LATE)], F32, name="sums")
-        negm = const.tile([P, len(LATE)], F32, name="negm")
-        wsb = const.tile([P, 1024], BF16, name="wsb")
-        gw = const.tile([P, 2, P, 4], BF16, name="gw", align_bytes=64)
-        wc = const.tile([P, 2 * P], U32, name="wc", align_bytes=64)
-        ws = const.tile([P, 2 * P], U8, name="ws", align_bytes=64)
+            nc.gpsimd.dma_start(out=gamma[:], in_=bn_gamma.rearrange("(o x) -> o x", x=1))
+            nc.gpsimd.dma_start(out=beta[:], in_=bn_beta.rearrange("(o x) -> o x", x=1))
+        stats = const.tile([P, 6 * VECTOR_STATS + 3 * len(SCALAR_STATS)], F32, name="stats")
+        scalar_triples = stats[:, 6 * VECTOR_STATS:].rearrange("p (k s) -> p k s", s=3)
+        nc.vector.memset(scalar_triples, float(GROUP_PIXELS))
+        totals = const.tile([P, len(SCALAR_STATS)], F32, name="totals")
+        w_tile = const.tile([P, 1024], BF16, name="w_tile")
+        w_grouped = const.tile([P, 2, P, PACK], BF16, name="w_grouped", align_bytes=64)
+        w_codes = const.tile([P, 2 * P], U32, name="w_codes", align_bytes=64)
+        w_scales = const.tile([P, 2 * P], U8, name="w_scales", align_bytes=64)
+        turned_w = psum.tile([P, 4, P], F32, name="turned_w", tag="sums")
 
-        def load_x(g):
-            xq[g] = xpool.tile([P, 2, 4, 256], BF16, name="xq")
-            dst = xq[g][:].rearrange("p b j n -> p b (j n)")
+        def load_query(g):
+            query_tile[g] = query_pool.tile([P, IMAGES, PACK, PIXELS], BF16, name="query_tile")
+            dst = query_tile[g][:].rearrange("p b j n -> p b (j n)")
             if g == 0:
-                for b in range(2):
-                    nc.sync.dma_start(out=dst[:, b], in_=q_v[g][:, b])
+                for b in range(IMAGES):
+                    nc.sync.dma_start(out=dst[:, b], in_=query_view[g][:, b])
             else:
-                nc.sync.dma_start(out=dst, in_=q_v[g])
+                nc.sync.dma_start(out=dst, in_=query_view[g])
 
-        def load_m(g):
-            mm[g] = mpool.tile([P, 2, 2, 512], BF16, name="mm")
-            nc.sync.dma_start(out=mm[g][:].rearrange("p b t k -> p b (t k)"), in_=m_v[g])
+        def load_memory(g):
+            memory_tile[g] = memory_pool.tile([P, IMAGES, 2, 512], BF16, name="memory_tile")
+            nc.sync.dma_start(out=memory_tile[g][:].rearrange("p b t k -> p b (t k)"), in_=memory_view[g])
 
-        def load_w():
-            nc.sync.dma_start(out=wsb[:], in_=conv_w)
-
-        wps = psum.tile([P, 4, P], F32, name="wps", tag="y")
-
-        def turn_w():
-            w32 = wsb[:].bitcast(F32)
+        def turn_weights():
+            words = w_tile[:].bitcast(F32)
             for h in range(2):
-                nc.tensor.transpose(wps[:, h, :], w32[:, h:256:2], ident[:])
+                nc.tensor.transpose(turned_w[:, h, :], words[:, h:256:2], ident[:])
             for u in range(2):
-                nc.tensor.transpose(wps[:, 2 + u, :], w32[:, 256 + P * u:256 + P * u + P], ident[:])
+                nc.tensor.transpose(turned_w[:, 2 + u, :], words[:, 256 + P * u:256 + P * u + P], ident[:])
 
-        def quant_w():
-            nc.vector.tensor_copy(out=gw[:].bitcast(F32), in_=wps[:].rearrange("p (a h) o -> p a o h", a=2))
-            nc.vector.quantize_mx(out=wc[:].bitcast(FP8X4), scales=ws[:], in_=gw[:].rearrange("p a o t -> p (a o t)"))
+        def quantise_weights():
+            nc.vector.tensor_copy(out=w_grouped[:].bitcast(F32),
+                                  in_=turned_w[:].rearrange("p (a h) o -> p a o h", a=2))
+            nc.vector.quantize_mx(out=w_codes[:].bitcast(FP8X4), scales=w_scales[:],
+                                  in_=w_grouped[:].rearrange("p a o t -> p (a o t)"))
 
-        def do_t1(g, b):
-            t1[(g, b)] = psum.tile([P, 4, P], F32, name="t1", tag="t1")
-            x32 = xq[g][:].bitcast(F32)
-            for j in range(4):
-                nc.tensor.transpose(t1[(g, b)][:, j, :], x32[:, b, j, :], ident[:])
+        def turn_query(g, b):
+            turned_q[(g, b)] = psum.tile([P, PACK, P], F32, name="turned_q", tag="turned_q")
+            words = query_tile[g][:].bitcast(F32)
+            for j in range(PACK):
+                nc.tensor.transpose(turned_q[(g, b)][:, j, :], words[:, b, j, :], ident[:])
 
-        def do_sq(g, b):
+        def sum_squares(g, b):
             if b == 0:
-                ss[g] = spool.tile([P, 4], F32, name="ss")
-            tb = t1[(g, b)][:].bitcast(BF16).rearrange("w j (p e) -> w j p e", e=2)
-            for e in range(2):
-                junk = jpool.tile([P, 4, P], BF16, name="junk")
-                nc.scalar.activation(out=junk[:], in_=tb[:, :, :, e], func=AF.Square,
-                                     accum_out=ss[g][:, 2 * b + e:2 * b + e + 1])
+                squares[g] = norm_pool.tile([P, 2 * IMAGES], F32, name="squares")
+            halves = turned_q[(g, b)][:].bitcast(BF16).rearrange("w j (p e) -> w j p e", e=2)
+            for parity in range(2):
+                unread = unread_pool.tile([P, PACK, P], BF16, name="unread")
+                nc.scalar.activation(out=unread[:], in_=halves[:, :, :, parity], func=AF.Square,
+                                     accum_out=squares[g][:, 2 * b + parity:2 * b + parity + 1])
 
-        def do_rsq(g):
-            rq[g] = spool.tile([P, 4], F32, name="rq")
-            nc.scalar.activation(out=rq[g][:], in_=ss[g][:], func=AF.Abs_reciprocal_sqrt)
-
-        def do_rc(g):
-            rr[g] = spool.tile([P, 4], F32, name="rr")
-            nc.gpsimd.tensor_scalar(out=rr[g][:], in0=rq[g][:], scalar1=1.0 / L2_EPS, scalar2=0.0,
+        def invert_norm(g):
+            inv_raw[g] = norm_pool.tile([P, 2 * IMAGES], F32, name="inv_raw")
+            nc.scalar.activation(out=inv_raw[g][:], in_=squares[g][:], func=AF.Abs_reciprocal_sqrt)
+            inv_norm[g] = norm_pool.tile([P, 2 * IMAGES], F32, name="inv_norm")
+            nc.gpsimd.tensor_scalar(out=inv_norm[g][:], in0=inv_raw[g][:], scalar1=1.0 / L2_EPS, scalar2=0.0,
                                     op0=ALU.min, op1=ALU.max)
 
-        def do_rb(g):
-            rbk[g] = psum.tile([P, 2, 2, P], F32, name="rbk", tag="rb")
-            for b in range(2):
-                for e in range(2):
-                    c = 2 * b + e
-                    nc.tensor.transpose(rbk[g][:, e, b, :], rr[g][:, c:c + 1].to_broadcast([P, P]), ident[:])
+        def spread_inv_norm(g):
+            spread[g] = psum.tile([P, 2, IMAGES, P], F32, name="spread", tag="spread")
+            for b in range(IMAGES):
+                for parity in range(2):
+                    column = 2 * b + parity
+                    nc.tensor.transpose(spread[g][:, parity, b, :],
+                                        inv_norm[g][:, column:column + 1].to_broadcast([P, P]), ident[:])
 
-        def do_bm(g):
-            gq[g] = gqpool.tile([P, 2, 256, 4], BF16, name="gq", align_bytes=64)
+        def normalise_query(g):
+            q_grouped[g] = q_pool.tile([P, IMAGES, PIXELS, PACK], BF16, name="q_grouped", align_bytes=64)
             nc.vector.tensor_tensor(
-                out=gq[g][:].rearrange("p b (w e) j -> p b w e j", e=2),
-                in0=xq[g][:].rearrange("p b j (w e) -> p b w e j", e=2),
-                in1=rbk[g][:].rearrange("p e b w -> p b w e").unsqueeze(4).to_broadcast([P, 2, P, 2, 4]),
+                out=q_grouped[g][:].rearrange("p b (w e) j -> p b w e j", e=2),
+                in0=query_tile[g][:].rearrange("p b j (w e) -> p b w e j", e=2),
+                in1=spread[g][:].rearrange("p e b w -> p b w e").unsqueeze(4).to_broadcast([P, IMAGES, P, 2, PACK]),
                 op=ALU.mult,
             )
 
-        def do_qq(g):
-            qc[g] = keep.tile([P, 512], U32, name="qc%d" % g, align_bytes=64)
-            qs[g] = keep.tile([P, 512], U8, name="qs%d" % g, align_bytes=64)
-            nc.vector.quantize_mx(out=qc[g][:].bitcast(FP8X4), scales=qs[g][:],
-                                  in_=gq[g][:].rearrange("p b n j -> p (b n j)"))
+        def quantise_query(g):
+            q_codes[g] = keep.tile([P, GROUP_PIXELS], U32, name="q_codes%d" % g, align_bytes=64)
+            q_scales[g] = keep.tile([P, GROUP_PIXELS], U8, name="q_scales%d" % g, align_bytes=64)
+            nc.vector.quantize_mx(out=q_codes[g][:].bitcast(FP8X4), scales=q_scales[g][:],
+                                  in_=q_grouped[g][:].rearrange("p b n j -> p (b n j)"))
 
-        def do_m1(g, b):
-            mt[(g, b)] = psum.tile([P, 2, 2, P], F32, name="mt", tag="mt")
-            m32 = mm[g][:].bitcast(F32)
+        def turn_memory(g, b):
+            turned_m[(g, b)] = psum.tile([P, 2, 2, P], F32, name="turned_m", tag="turned_m")
+            words = memory_tile[g][:].bitcast(F32)
             for t in range(2):
                 for u in range(2):
-                    nc.tensor.transpose(mt[(g, b)][:, u, t, :], m32[:, b, t, P * u:P * u + P], ident[:])
+                    nc.tensor.transpose(turned_m[(g, b)][:, u, t, :], words[:, b, t, P * u:P * u + P], ident[:])
 
-        def do_me(g, b):
+        def group_memory(g, b):
             if b == 0:
-                gm[g] = gmpool.tile([P, 2, 256, 4], BF16, name="gm", align_bytes=64)
+                m_grouped[g] = m_pool.tile([P, IMAGES, PIXELS, PACK], BF16, name="m_grouped", align_bytes=64)
             nc.scalar.copy(
-                out=gm[g][:].bitcast(F32)[:, b].rearrange("p (r t) u -> p r t u", t=2),
-                in_=mt[(g, b)][:].rearrange("p u t r -> p r t u"),
+                out=m_grouped[g][:].bitcast(F32)[:, b].rearrange("p (r t) u -> p r t u", t=2),
+                in_=turned_m[(g, b)][:].rearrange("p u t r -> p r t u"),
             )
 
-        def do_qm(g):
-            mc[g] = keep.tile([P, 512], U32, name="mc%d" % g, align_bytes=64)
-            ms[g] = keep.tile([P, 512], U8, name="ms%d" % g, align_bytes=64)
-            nc.vector.quantize_mx(out=mc[g][:].bitcast(FP8X4), scales=ms[g][:],
-                                  in_=gm[g][:].rearrange("p b n j -> p (b n j)"))
+        def quantise_memory(g):
+            m_codes[g] = keep.tile([P, GROUP_PIXELS], U32, name="m_codes%d" % g, align_bytes=64)
+            m_scales[g] = keep.tile([P, GROUP_PIXELS], U8, name="m_scales%d" % g, align_bytes=64)
+            nc.vector.quantize_mx(out=m_codes[g][:].bitcast(FP8X4), scales=m_scales[g][:],
+                                  in_=m_grouped[g][:].rearrange("p b n j -> p (b n j)"))
 
-        def do_mx(g, tag):
-            yb[g] = psum.tile([P, 512], F32, name="yb", tag=tag)
-            nc.tensor.matmul_mx(out=yb[g][:], lhsT=wc[:, 0:P].bitcast(FP8X4), lhsT_scale=ws[:, 0:P],
-                                rhs=qc[g][:].bitcast(FP8X4), rhs_scale=qs[g][:], start=True, stop=False)
-            nc.tensor.matmul_mx(out=yb[g][:], lhsT=wc[:, P:2 * P].bitcast(FP8X4), lhsT_scale=ws[:, P:2 * P],
-                                rhs=mc[g][:].bitcast(FP8X4), rhs_scale=ms[g][:], start=False, stop=True)
+        def multiply(g, kind):
+            sums[g] = psum.tile([P, GROUP_PIXELS], F32, name="sums", tag=kind)
+            bank_of[g] = kind
+            nc.tensor.matmul_mx(out=sums[g][:], lhsT=w_codes[:, 0:P].bitcast(FP8X4), lhsT_scale=w_scales[:, 0:P],
+                                rhs=q_codes[g][:].bitcast(FP8X4), rhs_scale=q_scales[g][:], start=True, stop=False)
+            nc.tensor.matmul_mx(out=sums[g][:], lhsT=w_codes[:, P:2 * P].bitcast(FP8X4),
+                                lhsT_scale=w_scales[:, P:2 * P],
+                                rhs=m_codes[g][:].bitcast(FP8X4), rhs_scale=m_scales[g][:], start=False, stop=True)
 
-        def do_bs(g):
-            if g in LATE:
-                k = LATE.index(g)
-                junk = jpool.tile([P, 512], BF16, name="junk")
-                nc.scalar.activation(out=junk[:], in_=yb[g][:], func=AF.Identity, accum_out=sums[:, k:k + 1])
-                nc.scalar.mul(out=late[:, k, 1:2], in_=sums[:, k:k + 1], mul=1.0 / 512.0)
-                nc.scalar.mul(out=negm[:, k:k + 1], in_=sums[:, k:k + 1], mul=-1.0 / 512.0)
-                junk = jpool.tile([P, 512], BF16, name="junk")
-                nc.scalar.activation(out=junk[:], in_=yb[g][:], func=AF.Square, bias=negm[:, k:k + 1],
-                                     accum_out=late[:, k, 2:3])
+        def first_bank(g):
+            if g < GROUPS - 4:
+                return "sums"
+            if g < GROUPS - 2:
+                return "turned_q"
+            return "turned_m"
+
+        def take_statistics(g):
+            if g in SCALAR_STATS:
+                k = SCALAR_STATS.index(g)
+                unread = unread_pool.tile([P, GROUP_PIXELS], BF16, name="unread")
+                nc.scalar.activation(out=unread[:], in_=sums[g][:], func=AF.Identity, accum_out=totals[:, k:k + 1])
+                nc.scalar.mul(out=scalar_triples[:, k, 1:2], in_=totals[:, k:k + 1], mul=1.0 / GROUP_PIXELS)
+                unread = unread_pool.tile([P, GROUP_PIXELS], BF16, name="unread")
+                nc.scalar.activation(out=unread[:], in_=sums[g][:], func=AF.Square, scale=-1.0,
+                                     bias=scalar_triples[:, k, 1:2], accum_out=scalar_triples[:, k, 2:3])
             else:
-                s = g if g < LATE[0] else g - len(LATE)
-                nc.vector.bn_stats(out=stats[:, 6 * s:6 * s + 6], in_=yb[g][:])
+                slot = g if g < SCALAR_STATS[0] else g - len(SCALAR_STATS)
+                nc.vector.bn_stats(out=stats[:, 6 * slot:6 * slot + 6], in_=sums[g][:])
 
-        def ok(g):
-            return 0 <= g < NG
+        def is_group(g):
+            return 0 <= g < GROUPS
 
-        first_tag = {12: "t1", 13: "t1", 14: "mt", 15: "mt"}
+        for rnd in range(-LOAD_QUERY_AHEAD, GROUPS + MX_BEHIND):
+            if is_group(rnd + LOAD_MEMORY_AHEAD):
+                load_memory(rnd + LOAD_MEMORY_AHEAD)
+            if is_group(rnd + LOAD_QUERY_AHEAD):
+                load_query(rnd + LOAD_QUERY_AHEAD)
+            if rnd == -LOAD_QUERY_AHEAD:
+                nc.sync.dma_start(out=w_tile[:], in_=conv_w)
+            if is_group(rnd + SPREAD_AHEAD) and rnd + SPREAD_AHEAD > 0:
+                spread_inv_norm(rnd + SPREAD_AHEAD)
+            if is_group(rnd - MX_BEHIND):
+                multiply(rnd - MX_BEHIND, first_bank(rnd - MX_BEHIND))
+            if rnd >= GROUPS - 1:
+                multiply(rnd - (GROUPS - 1), "spread")
+            if is_group(rnd + QUANTISE_AHEAD):
+                normalise_query(rnd + QUANTISE_AHEAD)
+            for b in range(IMAGES):
+                if is_group(rnd + SQUARE_AHEAD):
+                    turn_query(rnd + SQUARE_AHEAD, b)
+                    sum_squares(rnd + SQUARE_AHEAD, b)
+                if is_group(rnd + MEMORY_AHEAD):
+                    turn_memory(rnd + MEMORY_AHEAD, b)
+                    group_memory(rnd + MEMORY_AHEAD, b)
+                if rnd == -SPREAD_AHEAD - 1 and b == 0:
+                    spread_inv_norm(0)
+            if rnd == -SQUARE_AHEAD:
+                turn_weights()
+                quantise_weights()
+            if is_group(rnd + SQUARE_AHEAD):
+                invert_norm(rnd + SQUARE_AHEAD)
+            if is_group(rnd + QUANTISE_AHEAD):
+                quantise_memory(rnd + QUANTISE_AHEAD)
+                quantise_query(rnd + QUANTISE_AHEAD)
+            if is_group(rnd - MX_BEHIND):
+                take_statistics(rnd - MX_BEHIND)
 
-        for i in range(-7, NG + 1):
-            if ok(i + 6):
-                load_m(i + 6)
-            if ok(i + 7):
-                load_x(i + 7)
-            if i == -7:
-                load_w()
-            if i > -2 and ok(i + 2):
-                do_rb(i + 2)
-            if ok(i - 1):
-                do_mx(i - 1, first_tag.get(i - 1, "y"))
-            if i == 15:
-                do_mx(0, "rb")
-            if i == 16:
-                do_mx(1, "rb")
-            if ok(i + 1):
-                do_bm(i + 1)
-            for b in range(2):
-                if ok(i + 4):
-                    do_t1(i + 4, b)
-                    do_sq(i + 4, b)
-                if ok(i + 3):
-                    do_m1(i + 3, b)
-                    do_me(i + 3, b)
-                if i == -3 and b == 0:
-                    do_rb(0)
-            if i == -4:
-                turn_w()
-                quant_w()
-            if ok(i + 4):
-                do_rsq(i + 4)
-                do_rc(i + 4)
-            if i == 2:
-                nc.vector.tensor_copy(out=gam[:], in_=gam_b[:])
-                nc.vector.tensor_copy(out=bet[:], in_=bet_b[:])
-            if ok(i + 1):
-                do_qm(i + 1)
-                do_qq(i + 1)
-            if ok(i - 1):
-                do_bs(i - 1)
+        mean_var = const.tile([P, 2], F32, name="mean_var")
+        nc.vector.bn_aggr(out=mean_var[:], in_=stats[:])
+        neg_mean = const.tile([P, 1], F32, name="neg_mean")
+        nc.vector.tensor_scalar_mul(out=neg_mean[:], in0=mean_var[:, 0:1], scalar1=-1.0)
+        rstd = const.tile([P, 1], F32, name="rstd")
+        nc.scalar.activation(out=rstd[:], in_=mean_var[:, 1:2], func=AF.Abs_reciprocal_sqrt, bias=BN_EPS)
+        scale = const.tile([P, 1], F32, name="scale")
+        nc.scalar.mul(out=scale[:], in_=gamma[:], mul=rstd[:, 0:1])
+        shift = const.tile([P, 1], F32, name="shift")
+        nc.scalar.activation(out=shift[:], in_=scale[:], func=AF.Identity, bias=beta[:, 0:1], scale=neg_mean[:, 0:1])
 
-        mv = const.tile([P, 2], F32, name="mv")
-        nc.vector.bn_aggr(out=mv[:], in_=stats[:])
-        nmean = const.tile([P, 1], F32, name="nmean")
-        nc.vector.tensor_scalar_mul(out=nmean[:], in0=mv[:, 0:1], scalar1=-1.0)
-        rs = const.tile([P, 1], F32, name="rs")
-        nc.scalar.activation(out=rs[:], in_=mv[:, 1:2], func=AF.Abs_reciprocal_sqrt, bias=BN_EPS)
-        sc = const.tile([P, 1], F32, name="sc")
-        nc.scalar.mul(out=sc[:], in_=rs[:], mul=gam[:, 0:1])
-        bi = const.tile([P, 1], F32, name="bi")
-        nc.scalar.activation(out=bi[:], in_=sc[:], func=AF.Identity, bias=bet[:, 0:1], scale=nmean[:, 0:1])
-
-        order = [10, 11, 12, 13, 14, 15, 0, 1, 2, 3, 4, 5, 6, 7, 8, 9]
-        refill = ["y", "y", "t1", "t1", "mt", "mt", "rb", "rb"]
-        for n, g in enumerate(order):
-            st = keep.tile([P, 512], F32, name="st%d" % g)
+        in_psum = list(range(GROUPS - 6, GROUPS)) + [0, 1]
+        again = list(range(2, GROUPS - 6))
+        for n, g in enumerate(in_psum + again):
+            result = keep.tile([P, GROUP_PIXELS], F32, name="result%d" % g)
             if n % 3 == 1:
-                nc.vector.tensor_scalar(out=st[:], in0=yb[g][:], scalar1=sc[:, 0:1], scalar2=bi[:, 0:1],
+                nc.vector.tensor_scalar(out=result[:], in0=sums[g][:], scalar1=scale[:, 0:1], scalar2=shift[:, 0:1],
                                         op0=ALU.mult, op1=ALU.add)
-                nc.vector.tensor_scalar_max(out=st[:], in0=st[:], scalar1=0.0)
+                nc.vector.tensor_scalar_max(out=result[:], in0=result[:], scalar1=0.0)
             else:
-                nc.scalar.activation(out=st[:], in_=yb[g][:], func=AF.Relu, bias=bi[:, 0:1], scale=sc[:, 0:1])
-            nc.sync.dma_start(out=o_v[g], in_=st[:].rearrange("o (b n) -> o b n", b=2))
-            if n < 8:
-                do_mx(2 + n, refill[n])
+                nc.scalar.activation(out=result[:], in_=sums[g][:], func=AF.Relu, bias=shift[:, 0:1],
+                                     scale=scale[:, 0:1])
+            nc.sync.dma_start(out=out_view[g], in_=result[:].rearrange("o (b n) -> o b n", b=IMAGES))
+            if n < len(again):
+                multiply(again[n], bank_of[g])

from contextlib import ExitStack

import concourse.mybir as mybir
from concourse.masks import make_identity

F32 = mybir.dt.float32
BF16 = mybir.dt.bfloat16
U32 = mybir.dt.uint32
U8 = mybir.dt.uint8
FP8X4 = mybir.dt.float8_e4m3fn_x4
AF = mybir.ActivationFunctionType
ALU = mybir.AluOpType

P = 128
PACK = 4
GROUPS = 16
IMAGES = 2
PIXELS = 256
GROUP_PIXELS = IMAGES * PIXELS
FLOPS = 2 * 8192 * 1024 * 128

L2_EPS = 1e-12
BN_EPS = 1e-5

LOAD_QUERY_AHEAD = 7
LOAD_MEMORY_AHEAD = 6
SQUARE_AHEAD = 4
MEMORY_AHEAD = 3
SPREAD_AHEAD = 2
QUANTISE_AHEAD = 1
MX_BEHIND = 1

SCALAR_STATS = [10, 11, 12, 13]
VECTOR_STATS = GROUPS - len(SCALAR_STATS)


def tile_memory_sup_pb_t_kernel(tc, query, concat_memory, conv_w, bn_gamma, bn_beta, out):
    nc = tc.nc
    query_view = query.rearrange("(g b) (p j) h w -> g p b (j h w)", b=IMAGES, j=PACK)
    memory_view = concat_memory.rearrange("(g b p t) k -> g p b (t k)", b=IMAGES, p=P, t=2)
    out_view = out.rearrange("(g b) o h w -> g o b (h w)", b=IMAGES)

    with ExitStack() as ctx:
        ctx.enter_context(tc.manual_schedule())
        const = ctx.enter_context(tc.tile_pool(name="const", bufs=1))
        keep = ctx.enter_context(tc.tile_pool(name="keep", bufs=1))
        query_pool = ctx.enter_context(tc.tile_pool(name="query_pool", bufs=LOAD_QUERY_AHEAD - QUANTISE_AHEAD + 1))
        memory_pool = ctx.enter_context(tc.tile_pool(name="memory_pool", bufs=LOAD_MEMORY_AHEAD - MEMORY_AHEAD + 1))
        norm_pool = ctx.enter_context(tc.tile_pool(name="norm_pool", bufs=SQUARE_AHEAD - SPREAD_AHEAD + 1))
        m_pool = ctx.enter_context(tc.tile_pool(name="m_pool", bufs=MEMORY_AHEAD - QUANTISE_AHEAD + 2))
        q_pool = ctx.enter_context(tc.tile_pool(name="q_pool", bufs=2))
        unread_pool = ctx.enter_context(tc.tile_pool(name="unread_pool", bufs=2))
        psum = ctx.enter_context(tc.psum_pool(name="psum", bufs=2))

        query_tile = {}
        memory_tile = {}
        turned_q = {}
        turned_m = {}
        squares = {}
        inv_raw = {}
        inv_norm = {}
        spread = {}
        q_grouped = {}
        m_grouped = {}
        q_codes = {}
        q_scales = {}
        m_codes = {}
        m_scales = {}
        sums = {}
        bank_of = {}

        one = const.tile([P, 1], F32, name="one")
        nc.vector.memset(one[:], 1.0)
        warm = const.tile([P, 1], F32, name="warm")
        nc.scalar.activation(out=warm[:], in_=one[:], func=AF.Abs_reciprocal_sqrt)
        ident = const.tile([P, P], F32, name="ident")
        make_identity(nc, ident[:])
        gamma = const.tile([P, 1], BF16, name="gamma")
        beta = const.tile([P, 1], BF16, name="beta")
        with nc.allow_non_contiguous_dma(reason="one bn parameter per partition"):
            nc.gpsimd.dma_start(out=gamma[:], in_=bn_gamma.rearrange("(o x) -> o x", x=1))
            nc.gpsimd.dma_start(out=beta[:], in_=bn_beta.rearrange("(o x) -> o x", x=1))
        stats = const.tile([P, 6 * VECTOR_STATS + 3 * len(SCALAR_STATS)], F32, name="stats")
        scalar_triples = stats[:, 6 * VECTOR_STATS:].rearrange("p (k s) -> p k s", s=3)
        nc.vector.memset(scalar_triples, float(GROUP_PIXELS))
        totals = const.tile([P, len(SCALAR_STATS)], F32, name="totals")
        w_tile = const.tile([P, 1024], BF16, name="w_tile")
        w_grouped = const.tile([P, 2, P, PACK], BF16, name="w_grouped", align_bytes=64)
        w_codes = const.tile([P, 2 * P], U32, name="w_codes", align_bytes=64)
        w_scales = const.tile([P, 2 * P], U8, name="w_scales", align_bytes=64)
        turned_w = psum.tile([P, 4, P], F32, name="turned_w", tag="sums")

        def load_query(g):
            query_tile[g] = query_pool.tile([P, IMAGES, PACK, PIXELS], BF16, name="query_tile")
            dst = query_tile[g][:].rearrange("p b j n -> p b (j n)")
            if g == 0:
                for b in range(IMAGES):
                    nc.sync.dma_start(out=dst[:, b], in_=query_view[g][:, b])
            else:
                nc.sync.dma_start(out=dst, in_=query_view[g])

        def load_memory(g):
            memory_tile[g] = memory_pool.tile([P, IMAGES, 2, 512], BF16, name="memory_tile")
            nc.sync.dma_start(out=memory_tile[g][:].rearrange("p b t k -> p b (t k)"), in_=memory_view[g])

        def turn_weights():
            words = w_tile[:].bitcast(F32)
            for h in range(2):
                nc.tensor.transpose(turned_w[:, h, :], words[:, h:256:2], ident[:])
            for u in range(2):
                nc.tensor.transpose(turned_w[:, 2 + u, :], words[:, 256 + P * u:256 + P * u + P], ident[:])

        def quantise_weights():
            nc.vector.tensor_copy(out=w_grouped[:].bitcast(F32),
                                  in_=turned_w[:].rearrange("p (a h) o -> p a o h", a=2))
            nc.vector.quantize_mx(out=w_codes[:].bitcast(FP8X4), scales=w_scales[:],
                                  in_=w_grouped[:].rearrange("p a o t -> p (a o t)"))

        def turn_query(g, b):
            turned_q[(g, b)] = psum.tile([P, PACK, P], F32, name="turned_q", tag="turned_q")
            words = query_tile[g][:].bitcast(F32)
            for j in range(PACK):
                nc.tensor.transpose(turned_q[(g, b)][:, j, :], words[:, b, j, :], ident[:])

        def sum_squares(g, b):
            if b == 0:
                squares[g] = norm_pool.tile([P, 2 * IMAGES], F32, name="squares")
            halves = turned_q[(g, b)][:].bitcast(BF16).rearrange("w j (p e) -> w j p e", e=2)
            for parity in range(2):
                unread = unread_pool.tile([P, PACK, P], BF16, name="unread")
                nc.scalar.activation(out=unread[:], in_=halves[:, :, :, parity], func=AF.Square,
                                     accum_out=squares[g][:, 2 * b + parity:2 * b + parity + 1])

        def invert_norm(g):
            inv_raw[g] = norm_pool.tile([P, 2 * IMAGES], F32, name="inv_raw")
            nc.scalar.activation(out=inv_raw[g][:], in_=squares[g][:], func=AF.Abs_reciprocal_sqrt)
            inv_norm[g] = norm_pool.tile([P, 2 * IMAGES], F32, name="inv_norm")
            nc.gpsimd.tensor_scalar(out=inv_norm[g][:], in0=inv_raw[g][:], scalar1=1.0 / L2_EPS, scalar2=0.0,
                                    op0=ALU.min, op1=ALU.max)

        def spread_inv_norm(g):
            spread[g] = psum.tile([P, 2, IMAGES, P], F32, name="spread", tag="spread")
            for b in range(IMAGES):
                for parity in range(2):
                    column = 2 * b + parity
                    nc.tensor.transpose(spread[g][:, parity, b, :],
                                        inv_norm[g][:, column:column + 1].to_broadcast([P, P]), ident[:])

        def normalise_query(g):
            q_grouped[g] = q_pool.tile([P, IMAGES, PIXELS, PACK], BF16, name="q_grouped", align_bytes=64)
            nc.vector.tensor_tensor(
                out=q_grouped[g][:].rearrange("p b (w e) j -> p b w e j", e=2),
                in0=query_tile[g][:].rearrange("p b j (w e) -> p b w e j", e=2),
                in1=spread[g][:].rearrange("p e b w -> p b w e").unsqueeze(4).to_broadcast([P, IMAGES, P, 2, PACK]),
                op=ALU.mult,
            )

        def quantise_query(g):
            q_codes[g] = keep.tile([P, GROUP_PIXELS], U32, name="q_codes%d" % g, align_bytes=64)
            q_scales[g] = keep.tile([P, GROUP_PIXELS], U8, name="q_scales%d" % g, align_bytes=64)
            nc.vector.quantize_mx(out=q_codes[g][:].bitcast(FP8X4), scales=q_scales[g][:],
                                  in_=q_grouped[g][:].rearrange("p b n j -> p (b n j)"))

        def turn_memory(g, b):
            turned_m[(g, b)] = psum.tile([P, 2, 2, P], F32, name="turned_m", tag="turned_m")
            words = memory_tile[g][:].bitcast(F32)
            for t in range(2):
                for u in range(2):
                    nc.tensor.transpose(turned_m[(g, b)][:, u, t, :], words[:, b, t, P * u:P * u + P], ident[:])

        def group_memory(g, b):
            if b == 0:
                m_grouped[g] = m_pool.tile([P, IMAGES, PIXELS, PACK], BF16, name="m_grouped", align_bytes=64)
            nc.scalar.copy(
                out=m_grouped[g][:].bitcast(F32)[:, b].rearrange("p (r t) u -> p r t u", t=2),
                in_=turned_m[(g, b)][:].rearrange("p u t r -> p r t u"),
            )

        def quantise_memory(g):
            m_codes[g] = keep.tile([P, GROUP_PIXELS], U32, name="m_codes%d" % g, align_bytes=64)
            m_scales[g] = keep.tile([P, GROUP_PIXELS], U8, name="m_scales%d" % g, align_bytes=64)
            nc.vector.quantize_mx(out=m_codes[g][:].bitcast(FP8X4), scales=m_scales[g][:],
                                  in_=m_grouped[g][:].rearrange("p b n j -> p (b n j)"))

        def multiply(g, kind):
            sums[g] = psum.tile([P, GROUP_PIXELS], F32, name="sums", tag=kind)
            bank_of[g] = kind
            nc.tensor.matmul_mx(out=sums[g][:], lhsT=w_codes[:, 0:P].bitcast(FP8X4), lhsT_scale=w_scales[:, 0:P],
                                rhs=q_codes[g][:].bitcast(FP8X4), rhs_scale=q_scales[g][:], start=True, stop=False)
            nc.tensor.matmul_mx(out=sums[g][:], lhsT=w_codes[:, P:2 * P].bitcast(FP8X4),
                                lhsT_scale=w_scales[:, P:2 * P],
                                rhs=m_codes[g][:].bitcast(FP8X4), rhs_scale=m_scales[g][:], start=False, stop=True)

        def first_bank(g):
            if g < GROUPS - 4:
                return "sums"
            if g < GROUPS - 2:
                return "turned_q"
            return "turned_m"

        def take_statistics(g):
            if g in SCALAR_STATS:
                k = SCALAR_STATS.index(g)
                unread = unread_pool.tile([P, GROUP_PIXELS], BF16, name="unread")
                nc.scalar.activation(out=unread[:], in_=sums[g][:], func=AF.Identity, accum_out=totals[:, k:k + 1])
                nc.scalar.mul(out=scalar_triples[:, k, 1:2], in_=totals[:, k:k + 1], mul=1.0 / GROUP_PIXELS)
                unread = unread_pool.tile([P, GROUP_PIXELS], BF16, name="unread")
                nc.scalar.activation(out=unread[:], in_=sums[g][:], func=AF.Square, scale=-1.0,
                                     bias=scalar_triples[:, k, 1:2], accum_out=scalar_triples[:, k, 2:3])
            else:
                slot = g if g < SCALAR_STATS[0] else g - len(SCALAR_STATS)
                nc.vector.bn_stats(out=stats[:, 6 * slot:6 * slot + 6], in_=sums[g][:])

        def is_group(g):
            return 0 <= g < GROUPS

        for rnd in range(-LOAD_QUERY_AHEAD, GROUPS + MX_BEHIND):
            if is_group(rnd + LOAD_MEMORY_AHEAD):
                load_memory(rnd + LOAD_MEMORY_AHEAD)
            if is_group(rnd + LOAD_QUERY_AHEAD):
                load_query(rnd + LOAD_QUERY_AHEAD)
            if rnd == -LOAD_QUERY_AHEAD:
                nc.sync.dma_start(out=w_tile[:], in_=conv_w)
            if is_group(rnd + SPREAD_AHEAD) and rnd + SPREAD_AHEAD > 0:
                spread_inv_norm(rnd + SPREAD_AHEAD)
            if is_group(rnd - MX_BEHIND):
                multiply(rnd - MX_BEHIND, first_bank(rnd - MX_BEHIND))
            if rnd >= GROUPS - 1:
                multiply(rnd - (GROUPS - 1), "spread")
            if is_group(rnd + QUANTISE_AHEAD):
                normalise_query(rnd + QUANTISE_AHEAD)
            for b in range(IMAGES):
                if is_group(rnd + SQUARE_AHEAD):
                    turn_query(rnd + SQUARE_AHEAD, b)
                    sum_squares(rnd + SQUARE_AHEAD, b)
                if is_group(rnd + MEMORY_AHEAD):
                    turn_memory(rnd + MEMORY_AHEAD, b)
                    group_memory(rnd + MEMORY_AHEAD, b)
                if rnd == -SPREAD_AHEAD - 1 and b == 0:
                    spread_inv_norm(0)
            if rnd == -SQUARE_AHEAD:
                turn_weights()
                quantise_weights()
            if is_group(rnd + SQUARE_AHEAD):
                invert_norm(rnd + SQUARE_AHEAD)
            if is_group(rnd + QUANTISE_AHEAD):
                quantise_memory(rnd + QUANTISE_AHEAD)
                quantise_query(rnd + QUANTISE_AHEAD)
            if is_group(rnd - MX_BEHIND):
                take_statistics(rnd - MX_BEHIND)

        mean_var = const.tile([P, 2], F32, name="mean_var")
        nc.vector.bn_aggr(out=mean_var[:], in_=stats[:])
        neg_mean = const.tile([P, 1], F32, name="neg_mean")
        nc.vector.tensor_scalar_mul(out=neg_mean[:], in0=mean_var[:, 0:1], scalar1=-1.0)
        rstd = const.tile([P, 1], F32, name="rstd")
        nc.scalar.activation(out=rstd[:], in_=mean_var[:, 1:2], func=AF.Abs_reciprocal_sqrt, bias=BN_EPS)
        scale = const.tile([P, 1], F32, name="scale")
        nc.scalar.mul(out=scale[:], in_=gamma[:], mul=rstd[:, 0:1])
        shift = const.tile([P, 1], F32, name="shift")
        nc.scalar.activation(out=shift[:], in_=scale[:], func=AF.Identity, bias=beta[:, 0:1], scale=neg_mean[:, 0:1])

        in_psum = list(range(GROUPS - 6, GROUPS)) + [0, 1]
        again = list(range(2, GROUPS - 6))
        for n, g in enumerate(in_psum + again):
            result = keep.tile([P, GROUP_PIXELS], F32, name="result%d" % g)
            if n % 3 == 1:
                nc.vector.tensor_scalar(out=result[:], in0=sums[g][:], scalar1=scale[:, 0:1], scalar2=shift[:, 0:1],
                                        op0=ALU.mult, op1=ALU.add)
                nc.vector.tensor_scalar_max(out=result[:], in0=result[:], scalar1=0.0)
            else:
                nc.scalar.activation(out=result[:], in_=sums[g][:], func=AF.Relu, bias=shift[:, 0:1],
                                     scale=scale[:, 0:1])
            nc.sync.dma_start(out=out_view[g], in_=result[:].rearrange("o (b n) -> o b n", b=IMAGES))
            if n < len(again):
                multiply(again[n], bank_of[g])
